import numpy as np
import ml_dtypes

BF16 = ml_dtypes.bfloat16


def bf(x):
    return np.asarray(x, np.float32).astype(BF16)


def f32(x):
    return np.asarray(x, np.float32)


def f64(x):
    return np.asarray(x).astype(np.float64)


def striped(idx):
    return np.tile(idx.reshape(-1, 16).T, (8, 1))


S, D, H, E, N = 4096, 128, 512, 1024, 2048
OMEGA0 = 30.0


def uni(shape, bound):
    return np.random.uniform(-bound, bound, shape)


def setup_inputs():
    bnd = 0.75 * np.sqrt(6.0 / H) / OMEGA0
    xb = np.sqrt(6.0 / (H + E))
    return {
        "table": bf(uni((D, S), 1.0)),
        "w0": bf(uni((D, H), 0.5 / D)),
        "b0": f32(uni((H, 1), 0.3 / OMEGA0)),
        "w1": bf(uni((H, H), bnd)),
        "b1": f32(uni((H, 1), 0.3 / OMEGA0)),
        "w2": bf(uni((H, H), bnd)),
        "b2": f32(uni((H, 1), 0.3 / OMEGA0)),
        "wout": bf(uni((H, E), xb)),
        "bout": f32(0.1 * np.random.standard_normal((E, 1))),
        "offs": striped(np.random.permutation(np.tile(np.arange(S), 2))[:N]),
    }


def reference(table, w0, b0, w1, b1, w2, b2, wout, bout, offs):
    idx = offs[:16].T.reshape(-1)
    h = np.sin(OMEGA0 * (f64(w0).T @ f64(table)[:, idx] + f64(b0)))
    h = np.sin(OMEGA0 * (f64(w1).T @ h + f64(b1)))
    h = np.sin(OMEGA0 * (f64(w2).T @ h + f64(b2)))
    return f64(wout).T @ h + f64(bout)

@@ -1,0 +1,145 @@
+import math
+
+import concourse.mybir as mybir
+from concourse.masks import make_identity
+
+BF16 = mybir.dt.bfloat16
+F32 = mybir.dt.float32
+I32 = mybir.dt.int32
+U16 = mybir.dt.uint16
+ADD = mybir.AluOpType.add
+MULT = mybir.AluOpType.mult
+SIN = mybir.ActivationFunctionType.Sin
+IDENTITY = mybir.ActivationFunctionType.Identity
+
+P = 128
+WORDS, COORDS, HIDDEN, EMBED, TOKENS = 4096, 128, 512, 1024, 2048
+PIECE = 512
+N_PIECES = TOKENS // PIECE
+HID_BLOCKS = HIDDEN // P
+EMB_BLOCKS = EMBED // P
+SINE_LAYERS = 3
+BIAS_ROWS = SINE_LAYERS * HID_BLOCKS + EMB_BLOCKS
+OMEGA0 = 30.0
+PERIOD = 2.0 * math.pi / OMEGA0
+
+FLOPS = 2 * TOKENS * (COORDS * HIDDEN + 2 * HIDDEN * HIDDEN + HIDDEN * EMBED)
+
+
+def tile_implicitembedding_b_kernel(
+    tc, table, w0, b0, w1, b1, w2, b2, wout, bout, offs, out
+):
+    nc = tc.nc
+    with (
+        tc.tile_pool(name="held", bufs=1) as held,
+        tc.tile_pool(name="hidden", bufs=SINE_LAYERS * N_PIECES * HID_BLOCKS) as hidden,
+        tc.tile_pool(name="work", bufs=4) as work,
+        tc.psum_pool(name="psum", bufs=8) as psum,
+    ):
+        offsets = held.tile([P, TOKENS // 16], U16, name="offsets")
+        nc.sync.dma_start(offsets[:], offs)
+        table_sb = held.tile([P, WORDS], BF16, name="table_sb")
+        nc.sync.dma_start(table_sb[:], table)
+        w0_sb = held.tile([P, HIDDEN], BF16, name="w0_sb")
+        nc.scalar.dma_start(w0_sb[:], w0)
+
+        bias_rows = held.tile([BIAS_ROWS, P], F32, name="bias_rows")
+        row = 0
+        for bias in (b0, b1, b2, bout):
+            blocks = bias.shape[0] // P
+            nc.scalar.dma_start(
+                bias_rows[row : row + blocks, :],
+                bias.rearrange("(t p) one -> t (p one)", p=P),
+            )
+            row += blocks
+
+        w1_sb = held.tile([P, HID_BLOCKS, HIDDEN], BF16, name="w1_sb")
+        nc.sync.dma_start(w1_sb[:], w1.rearrange("(kb p) m -> p kb m", p=P))
+        w2_sb = held.tile([P, HID_BLOCKS, HIDDEN], BF16, name="w2_sb")
+        nc.sync.dma_start(w2_sb[:], w2.rearrange("(kb p) m -> p kb m", p=P))
+        wout_sb = held.tile([P, HID_BLOCKS, EMBED], BF16, name="wout_sb")
+        nc.sync.dma_start(wout_sb[:], wout.rearrange("(kb p) e -> p kb e", p=P))
+
+        identity = held.tile([BIAS_ROWS, BIAS_ROWS], F32, name="identity")
+        make_identity(nc, identity[:])
+        flipped = psum.tile([P, PIECE], F32, name="acc")
+        nc.tensor.matmul(
+            flipped[:, 0:BIAS_ROWS], bias_rows[:], identity[:], start=True, stop=True
+        )
+        bias_cols = held.tile([P, BIAS_ROWS], F32, name="bias_cols")
+        nc.vector.tensor_copy(bias_cols[:], flipped[:, 0:BIAS_ROWS])
+        bias_times_omega = held.tile([P, BIAS_ROWS], F32, name="bias_times_omega")
+        nc.vector.tensor_scalar(
+            bias_times_omega[:], flipped[:, 0:BIAS_ROWS], OMEGA0, None, op0=MULT
+        )
+
+        def sine(acc, column):
+            turns = work.tile([P, PIECE], I32, name="turns")
+            nc.vector.tensor_scalar(
+                turns[:], acc[:], bias_cols[:, column : column + 1], 1.0 / PERIOD,
+                op0=ADD, op1=MULT,
+            )
+            rest = work.tile([P, PIECE], F32, name="rest")
+            nc.vector.scalar_tensor_tensor(
+                rest[:], turns[:], -PERIOD, acc[:], op0=MULT, op1=ADD
+            )
+            h = hidden.tile([P, PIECE], BF16, name="h")
+            nc.scalar.activation(
+                h[:], rest[:], SIN,
+                bias=bias_times_omega[:, column : column + 1], scale=OMEGA0,
+            )
+            return h
+
+        def first_layer(piece):
+            h_out = []
+            for mb in range(HID_BLOCKS):
+                acc = psum.tile([P, PIECE], F32, name="acc")
+                nc.tensor.matmul(
+                    acc[:],
+                    w0_sb[:, mb * P : (mb + 1) * P],
+                    table_sb[:].indirect(
+                        offsets[:, piece * (PIECE // 16) : (piece + 1) * (PIECE // 16)]
+                    ),
+                    start=True, stop=True,
+                )
+                h_out.append(sine(acc, mb))
+            return h_out
+
+        def hidden_layer(layer, w_sb, h_in):
+            h_out = []
+            for mb in range(HID_BLOCKS):
+                acc = psum.tile([P, PIECE], F32, name="acc")
+                for kb in range(HID_BLOCKS):
+                    nc.tensor.matmul(
+                        acc[:], w_sb[:, kb, mb * P : (mb + 1) * P], h_in[kb][:],
+                        start=(kb == 0), stop=(kb == HID_BLOCKS - 1),
+                    )
+                h_out.append(sine(acc, layer * HID_BLOCKS + mb))
+            return h_out
+
+        def projection(piece, h_in):
+            for eb in range(EMB_BLOCKS):
+                acc = psum.tile([P, PIECE], F32, name="acc")
+                for kb in range(HID_BLOCKS):
+                    nc.tensor.matmul(
+                        acc[:], wout_sb[:, kb, eb * P : (eb + 1) * P], h_in[kb][:],
+                        start=(kb == 0), stop=(kb == HID_BLOCKS - 1),
+                    )
+                column = SINE_LAYERS * HID_BLOCKS + eb
+                emb = work.tile([P, PIECE], F32, name="emb")
+                nc.scalar.activation(
+                    emb[:], acc[:], IDENTITY,
+                    bias=bias_cols[:, column : column + 1], scale=1.0,
+                )
+                nc.sync.dma_start(
+                    out[eb * P : (eb + 1) * P, piece * PIECE : (piece + 1) * PIECE],
+                    emb[:],
+                )
+
+        for first in range(0, N_PIECES, 2):
+            pair = (first, first + 1)
+            h = {piece: first_layer(piece) for piece in pair}
+            h = {piece: hidden_layer(1, w1_sb, h[piece]) for piece in pair}
+            h = {piece: hidden_layer(2, w2_sb, h[piece]) for piece in pair}
+            for piece in pair:
+                projection(piece, h[piece])

@@ -136,10 +136,20 @@ def tile_implicitembedding_b_kernel(
                     emb[:],
                 )
 
-        for first in range(0, N_PIECES, 2):
-            pair = (first, first + 1)
-            h = {piece: first_layer(piece) for piece in pair}
-            h = {piece: hidden_layer(1, w1_sb, h[piece]) for piece in pair}
-            h = {piece: hidden_layer(2, w2_sb, h[piece]) for piece in pair}
-            for piece in pair:
-                projection(piece, h[piece])
+        h = {}
+        for piece in (0, 1):
+            h[piece] = first_layer(piece)
+        for piece in (0, 1):
+            h[piece] = hidden_layer(1, w1_sb, h[piece])
+        for piece in (0, 1):
+            h[piece] = hidden_layer(2, w2_sb, h[piece])
+        for piece in (2, 3):
+            h[piece] = first_layer(piece)
+        projection(0, h[0])
+        for piece in (2, 3):
+            h[piece] = hidden_layer(1, w1_sb, h[piece])
+        projection(1, h[1])
+        for piece in (2, 3):
+            h[piece] = hidden_layer(2, w2_sb, h[piece])
+        projection(2, h[2])
+        projection(3, h[3])

@@ -105,51 +105,42 @@ def tile_implicitembedding_b_kernel(
                 h_out.append(sine(acc, mb))
             return h_out
 
-        def hidden_layer(layer, w_sb, h_in):
-            h_out = []
-            for mb in range(HID_BLOCKS):
-                acc = psum.tile([P, PIECE], F32, name="acc")
-                for kb in range(HID_BLOCKS):
+        def dense(w_sb, first_block, n_blocks, h_in):
+            accs = [psum.tile([P, PIECE], F32, name="acc") for bank in range(n_blocks)]
+            for kb in range(HID_BLOCKS):
+                for bank, acc in enumerate(accs):
+                    ob = first_block + bank
                     nc.tensor.matmul(
-                        acc[:], w_sb[:, kb, mb * P : (mb + 1) * P], h_in[kb][:],
+                        acc[:], w_sb[:, kb, ob * P : (ob + 1) * P], h_in[kb][:],
                         start=(kb == 0), stop=(kb == HID_BLOCKS - 1),
                     )
-                h_out.append(sine(acc, layer * HID_BLOCKS + mb))
-            return h_out
+            return accs
+
+        def hidden_layer(layer, w_sb, h_in):
+            accs = dense(w_sb, 0, HID_BLOCKS, h_in)
+            return [sine(acc, layer * HID_BLOCKS + mb) for mb, acc in enumerate(accs)]
+
+        def store(piece, eb, acc):
+            column = SINE_LAYERS * HID_BLOCKS + eb
+            emb = work.tile([P, PIECE], F32, name="emb")
+            nc.scalar.activation(
+                emb[:], acc[:], IDENTITY, bias=bias_cols[:, column : column + 1], scale=1.0
+            )
+            nc.sync.dma_start(
+                out[eb * P : (eb + 1) * P, piece * PIECE : (piece + 1) * PIECE], emb[:]
+            )
 
         def projection(piece, h_in):
-            for eb in range(EMB_BLOCKS):
-                acc = psum.tile([P, PIECE], F32, name="acc")
-                for kb in range(HID_BLOCKS):
-                    nc.tensor.matmul(
-                        acc[:], wout_sb[:, kb, eb * P : (eb + 1) * P], h_in[kb][:],
-                        start=(kb == 0), stop=(kb == HID_BLOCKS - 1),
-                    )
-                column = SINE_LAYERS * HID_BLOCKS + eb
-                emb = work.tile([P, PIECE], F32, name="emb")
-                nc.scalar.activation(
-                    emb[:], acc[:], IDENTITY,
-                    bias=bias_cols[:, column : column + 1], scale=1.0,
-                )
-                nc.sync.dma_start(
-                    out[eb * P : (eb + 1) * P, piece * PIECE : (piece + 1) * PIECE],
-                    emb[:],
-                )
+            half = EMB_BLOCKS // 2
+            for eb, acc in enumerate(dense(wout_sb, 0, half, h_in)):
+                store(piece, eb, acc)
+            for eb in range(half, EMB_BLOCKS):
+                store(piece, eb, dense(wout_sb, eb, 1, h_in)[0])
 
-        h = {}
-        for piece in (0, 1):
-            h[piece] = first_layer(piece)
-        for piece in (0, 1):
-            h[piece] = hidden_layer(1, w1_sb, h[piece])
-        for piece in (0, 1):
-            h[piece] = hidden_layer(2, w2_sb, h[piece])
-        for piece in (2, 3):
-            h[piece] = first_layer(piece)
-        projection(0, h[0])
-        for piece in (2, 3):
-            h[piece] = hidden_layer(1, w1_sb, h[piece])
-        projection(1, h[1])
-        for piece in (2, 3):
-            h[piece] = hidden_layer(2, w2_sb, h[piece])
-        projection(2, h[2])
-        projection(3, h[3])
+        for first in range(0, N_PIECES, 2):
+            pair = (first, first + 1)
+            h = {piece: first_layer(piece) for piece in pair}
+            h = {piece: hidden_layer(1, w1_sb, h[piece]) for piece in pair}
+            h = {piece: hidden_layer(2, w2_sb, h[piece]) for piece in pair}
+            for piece in pair:
+                projection(piece, h[piece])

@@ -19,6 +19,7 @@ N_PIECES = TOKENS // PIECE
 HID_BLOCKS = HIDDEN // P
 EMB_BLOCKS = EMBED // P
 SINE_LAYERS = 3
+BLOCKS_A_HALF = EMB_BLOCKS // 2
 BIAS_ROWS = SINE_LAYERS * HID_BLOCKS + EMB_BLOCKS
 OMEGA0 = 30.0
 PERIOD = 2.0 * math.pi / OMEGA0
@@ -130,17 +131,32 @@ def tile_implicitembedding_b_kernel(
                 out[eb * P : (eb + 1) * P, piece * PIECE : (piece + 1) * PIECE], emb[:]
             )
 
-        def projection(piece, h_in):
-            half = EMB_BLOCKS // 2
-            for eb, acc in enumerate(dense(wout_sb, 0, half, h_in)):
-                store(piece, eb, acc)
-            for eb in range(half, EMB_BLOCKS):
-                store(piece, eb, dense(wout_sb, eb, 1, h_in)[0])
+        def projection(piece, half, h_in):
+            first_block = half * BLOCKS_A_HALF
+            if half == 0:
+                for bank, acc in enumerate(dense(wout_sb, first_block, BLOCKS_A_HALF, h_in)):
+                    store(piece, first_block + bank, acc)
+            else:
+                for eb in range(first_block, first_block + BLOCKS_A_HALF):
+                    store(piece, eb, dense(wout_sb, eb, 1, h_in)[0])
 
-        for first in range(0, N_PIECES, 2):
-            pair = (first, first + 1)
-            h = {piece: first_layer(piece) for piece in pair}
-            h = {piece: hidden_layer(1, w1_sb, h[piece]) for piece in pair}
-            h = {piece: hidden_layer(2, w2_sb, h[piece]) for piece in pair}
-            for piece in pair:
-                projection(piece, h[piece])
+        h = {}
+        for piece in (0, 1):
+            h[piece] = first_layer(piece)
+        for piece in (0, 1):
+            h[piece] = hidden_layer(1, w1_sb, h[piece])
+        for piece in (0, 1):
+            h[piece] = hidden_layer(2, w2_sb, h[piece])
+        projection(0, 0, h[0])
+        for piece in (2, 3):
+            h[piece] = first_layer(piece)
+        projection(0, 1, h[0])
+        for piece in (2, 3):
+            h[piece] = hidden_layer(1, w1_sb, h[piece])
+        projection(1, 0, h[1])
+        for piece in (2, 3):
+            h[piece] = hidden_layer(2, w2_sb, h[piece])
+        projection(1, 1, h[1])
+        for piece in (2, 3):
+            for half in (0, 1):
+                projection(piece, half, h[piece])

@@ -19,6 +19,7 @@ N_PIECES = TOKENS // PIECE
 HID_BLOCKS = HIDDEN // P
 EMB_BLOCKS = EMBED // P
 SINE_LAYERS = 3
+WARM_UP_MATMULS = 10
 BLOCKS_A_HALF = EMB_BLOCKS // 2
 BIAS_ROWS = SINE_LAYERS * HID_BLOCKS + EMB_BLOCKS
 OMEGA0 = 30.0
@@ -60,6 +61,12 @@ def tile_implicitembedding_b_kernel(
         nc.sync.dma_start(w2_sb[:], w2.rearrange("(kb p) m -> p kb m", p=P))
         wout_sb = held.tile([P, HID_BLOCKS, EMBED], BF16, name="wout_sb")
         nc.sync.dma_start(wout_sb[:], wout.rearrange("(kb p) e -> p kb e", p=P))
+
+        zeros = held.tile([P, PIECE], BF16, name="zeros")
+        nc.vector.memset(zeros[:], 0.0)
+        warm = psum.tile([P, PIECE], F32, name="acc")
+        for repeat in range(WARM_UP_MATMULS):
+            nc.tensor.matmul(warm[:], zeros[:, 0:P], zeros[:], start=True, stop=True)
 
         identity = held.tile([BIAS_ROWS, BIAS_ROWS], F32, name="identity")
         make_identity(nc, identity[:])

@@ -1,16 +1,12 @@
-import math
-
 import concourse.mybir as mybir
 from concourse.masks import make_identity
 
 BF16 = mybir.dt.bfloat16
 F32 = mybir.dt.float32
-I32 = mybir.dt.int32
 U16 = mybir.dt.uint16
 ADD = mybir.AluOpType.add
 MULT = mybir.AluOpType.mult
 SIN = mybir.ActivationFunctionType.Sin
-IDENTITY = mybir.ActivationFunctionType.Identity
 
 P = 128
 WORDS, COORDS, HIDDEN, EMBED, TOKENS = 4096, 128, 512, 1024, 2048
@@ -23,7 +19,6 @@ WARM_UP_MATMULS = 10
 BLOCKS_A_HALF = EMB_BLOCKS // 2
 BIAS_ROWS = SINE_LAYERS * HID_BLOCKS + EMB_BLOCKS
 OMEGA0 = 30.0
-PERIOD = 2.0 * math.pi / OMEGA0
 
 FLOPS = 2 * TOKENS * (COORDS * HIDDEN + 2 * HIDDEN * HIDDEN + HIDDEN * EMBED)
 
@@ -82,18 +77,9 @@ def tile_implicitembedding_b_kernel(
         )
 
         def sine(acc, column):
-            turns = work.tile([P, PIECE], I32, name="turns")
-            nc.vector.tensor_scalar(
-                turns[:], acc[:], bias_cols[:, column : column + 1], 1.0 / PERIOD,
-                op0=ADD, op1=MULT,
-            )
-            rest = work.tile([P, PIECE], F32, name="rest")
-            nc.vector.scalar_tensor_tensor(
-                rest[:], turns[:], -PERIOD, acc[:], op0=MULT, op1=ADD
-            )
             h = hidden.tile([P, PIECE], BF16, name="h")
             nc.scalar.activation(
-                h[:], rest[:], SIN,
+                h[:], acc[:], SIN,
                 bias=bias_times_omega[:, column : column + 1], scale=OMEGA0,
             )
             return h
@@ -131,8 +117,8 @@ def tile_implicitembedding_b_kernel(
         def store(piece, eb, acc):
             column = SINE_LAYERS * HID_BLOCKS + eb
             emb = work.tile([P, PIECE], F32, name="emb")
-            nc.scalar.activation(
-                emb[:], acc[:], IDENTITY, bias=bias_cols[:, column : column + 1], scale=1.0
+            nc.vector.tensor_scalar(
+                emb[:], acc[:], bias_cols[:, column : column + 1], None, op0=ADD
             )
             nc.sync.dma_start(
                 out[eb * P : (eb + 1) * P, piece * PIECE : (piece + 1) * PIECE], emb[:]

@@ -17,6 +17,8 @@ EMB_BLOCKS = EMBED // P
 SINE_LAYERS = 3
 WARM_UP_MATMULS = 10
 BLOCKS_A_HALF = EMB_BLOCKS // 2
+STORES_IN_FLIGHT = 12
+LAST_WIDTH = 128
 BIAS_ROWS = SINE_LAYERS * HID_BLOCKS + EMB_BLOCKS
 OMEGA0 = 30.0
 
@@ -30,7 +32,7 @@ def tile_implicitembedding_b_kernel(
     with (
         tc.tile_pool(name="held", bufs=1) as held,
         tc.tile_pool(name="hidden", bufs=SINE_LAYERS * N_PIECES * HID_BLOCKS) as hidden,
-        tc.tile_pool(name="work", bufs=4) as work,
+        tc.tile_pool(name="work", bufs=STORES_IN_FLIGHT) as work,
         tc.psum_pool(name="psum", bufs=8) as psum,
     ):
         offsets = held.tile([P, TOKENS // 16], U16, name="offsets")
@@ -114,24 +116,38 @@ def tile_implicitembedding_b_kernel(
             accs = dense(w_sb, 0, HID_BLOCKS, h_in)
             return [sine(acc, layer * HID_BLOCKS + mb) for mb, acc in enumerate(accs)]
 
-        def store(piece, eb, acc):
+        def store(piece, eb, acc, first, width):
             column = SINE_LAYERS * HID_BLOCKS + eb
             emb = work.tile([P, PIECE], F32, name="emb")
             nc.vector.tensor_scalar(
-                emb[:], acc[:], bias_cols[:, column : column + 1], None, op0=ADD
+                emb[:, 0:width], acc[:, 0:width], bias_cols[:, column : column + 1], None,
+                op0=ADD,
             )
+            token = piece * PIECE + first
             nc.sync.dma_start(
-                out[eb * P : (eb + 1) * P, piece * PIECE : (piece + 1) * PIECE], emb[:]
+                out[eb * P : (eb + 1) * P, token : token + width], emb[:, 0:width]
             )
 
-        def projection(piece, half, h_in):
+        def projection(piece, half, h_in, n_blocks=BLOCKS_A_HALF):
             first_block = half * BLOCKS_A_HALF
             if half == 0:
                 for bank, acc in enumerate(dense(wout_sb, first_block, BLOCKS_A_HALF, h_in)):
-                    store(piece, first_block + bank, acc)
+                    store(piece, first_block + bank, acc, 0, PIECE)
             else:
-                for eb in range(first_block, first_block + BLOCKS_A_HALF):
-                    store(piece, eb, dense(wout_sb, eb, 1, h_in)[0])
+                for eb in range(first_block, first_block + n_blocks):
+                    store(piece, eb, dense(wout_sb, eb, 1, h_in)[0], 0, PIECE)
+
+        def last_block(piece, eb, h_in):
+            for first in range(0, PIECE, LAST_WIDTH):
+                acc = psum.tile([P, PIECE], F32, name="acc")
+                for kb in range(HID_BLOCKS):
+                    nc.tensor.matmul(
+                        acc[:, 0:LAST_WIDTH],
+                        wout_sb[:, kb, eb * P : (eb + 1) * P],
+                        h_in[kb][:, first : first + LAST_WIDTH],
+                        start=(kb == 0), stop=(kb == HID_BLOCKS - 1),
+                    )
+                store(piece, eb, acc, first, LAST_WIDTH)
 
         h = {}
         for piece in (0, 1):
@@ -150,6 +166,8 @@ def tile_implicitembedding_b_kernel(
         for piece in (2, 3):
             h[piece] = hidden_layer(2, w2_sb, h[piece])
         projection(1, 1, h[1])
-        for piece in (2, 3):
-            for half in (0, 1):
-                projection(piece, half, h[piece])
+        projection(2, 0, h[2])
+        projection(2, 1, h[2])
+        projection(3, 0, h[3])
+        projection(3, 1, h[3], BLOCKS_A_HALF - 1)
+        last_block(3, EMB_BLOCKS - 1, h[3])

@@ -15,7 +15,6 @@ N_PIECES = TOKENS // PIECE
 HID_BLOCKS = HIDDEN // P
 EMB_BLOCKS = EMBED // P
 SINE_LAYERS = 3
-WARM_UP_MATMULS = 10
 BLOCKS_A_HALF = EMB_BLOCKS // 2
 STORES_IN_FLIGHT = 12
 LAST_WIDTH = 128
@@ -35,6 +34,16 @@ def tile_implicitembedding_b_kernel(
         tc.tile_pool(name="work", bufs=STORES_IN_FLIGHT) as work,
         tc.psum_pool(name="psum", bufs=8) as psum,
     ):
+        bias_rows = held.tile([BIAS_ROWS, P], F32, name="bias_rows")
+        row = 0
+        for bias in (b0, b1, b2, bout):
+            blocks = bias.shape[0] // P
+            nc.sync.dma_start(
+                bias_rows[row : row + blocks, :],
+                bias.rearrange("(t p) one -> t (p one)", p=P),
+            )
+            row += blocks
+
         offsets = held.tile([P, TOKENS // 16], U16, name="offsets")
         nc.sync.dma_start(offsets[:], offs)
         table_sb = held.tile([P, WORDS], BF16, name="table_sb")
@@ -42,28 +51,12 @@ def tile_implicitembedding_b_kernel(
         w0_sb = held.tile([P, HIDDEN], BF16, name="w0_sb")
         nc.scalar.dma_start(w0_sb[:], w0)
 
-        bias_rows = held.tile([BIAS_ROWS, P], F32, name="bias_rows")
-        row = 0
-        for bias in (b0, b1, b2, bout):
-            blocks = bias.shape[0] // P
-            nc.scalar.dma_start(
-                bias_rows[row : row + blocks, :],
-                bias.rearrange("(t p) one -> t (p one)", p=P),
-            )
-            row += blocks
-
         w1_sb = held.tile([P, HID_BLOCKS, HIDDEN], BF16, name="w1_sb")
         nc.sync.dma_start(w1_sb[:], w1.rearrange("(kb p) m -> p kb m", p=P))
         w2_sb = held.tile([P, HID_BLOCKS, HIDDEN], BF16, name="w2_sb")
         nc.sync.dma_start(w2_sb[:], w2.rearrange("(kb p) m -> p kb m", p=P))
         wout_sb = held.tile([P, HID_BLOCKS, EMBED], BF16, name="wout_sb")
         nc.sync.dma_start(wout_sb[:], wout.rearrange("(kb p) e -> p kb e", p=P))
-
-        zeros = held.tile([P, PIECE], BF16, name="zeros")
-        nc.vector.memset(zeros[:], 0.0)
-        warm = psum.tile([P, PIECE], F32, name="acc")
-        for repeat in range(WARM_UP_MATMULS):
-            nc.tensor.matmul(warm[:], zeros[:, 0:P], zeros[:], start=True, stop=True)
 
         identity = held.tile([BIAS_ROWS, BIAS_ROWS], F32, name="identity")
         make_identity(nc, identity[:])

@@ -156,10 +156,10 @@ def tile_implicitembedding_b_kernel(
         for piece in (2, 3):
             h[piece] = hidden_layer(1, w1_sb, h[piece])
         projection(1, 0, h[1])
-        for piece in (2, 3):
-            h[piece] = hidden_layer(2, w2_sb, h[piece])
+        h[2] = hidden_layer(2, w2_sb, h[2])
         projection(1, 1, h[1])
         projection(2, 0, h[2])
+        h[3] = hidden_layer(2, w2_sb, h[3])
         projection(2, 1, h[2])
         projection(3, 0, h[3])
         projection(3, 1, h[3], BLOCKS_A_HALF - 1)

@@ -15,9 +15,8 @@ N_PIECES = TOKENS // PIECE
 HID_BLOCKS = HIDDEN // P
 EMB_BLOCKS = EMBED // P
 SINE_LAYERS = 3
+PSUM_BANKS = 8
 BLOCKS_A_HALF = EMB_BLOCKS // 2
-STORES_IN_FLIGHT = 12
-LAST_WIDTH = 128
 BIAS_ROWS = SINE_LAYERS * HID_BLOCKS + EMB_BLOCKS
 OMEGA0 = 30.0
 
@@ -31,8 +30,8 @@ def tile_implicitembedding_b_kernel(
     with (
         tc.tile_pool(name="held", bufs=1) as held,
         tc.tile_pool(name="hidden", bufs=SINE_LAYERS * N_PIECES * HID_BLOCKS) as hidden,
-        tc.tile_pool(name="work", bufs=STORES_IN_FLIGHT) as work,
-        tc.psum_pool(name="psum", bufs=8) as psum,
+        tc.tile_pool(name="work", bufs=PSUM_BANKS) as work,
+        tc.psum_pool(name="psum", bufs=PSUM_BANKS) as psum,
     ):
         bias_rows = held.tile([BIAS_ROWS, P], F32, name="bias_rows")
         row = 0
@@ -72,12 +71,12 @@ def tile_implicitembedding_b_kernel(
         )
 
         def sine(acc, column):
-            h = hidden.tile([P, PIECE], BF16, name="h")
+            h_block = hidden.tile([P, PIECE], BF16, name="h_block")
             nc.scalar.activation(
-                h[:], acc[:], SIN,
+                h_block[:], acc[:], SIN,
                 bias=bias_times_omega[:, column : column + 1], scale=OMEGA0,
             )
-            return h
+            return h_block
 
         def first_layer(piece):
             h_out = []
@@ -94,53 +93,32 @@ def tile_implicitembedding_b_kernel(
                 h_out.append(sine(acc, mb))
             return h_out
 
-        def dense(w_sb, first_block, n_blocks, h_in):
-            accs = [psum.tile([P, PIECE], F32, name="acc") for bank in range(n_blocks)]
+        def dense_block(w_sb, ob, h_in):
+            acc = psum.tile([P, PIECE], F32, name="acc")
             for kb in range(HID_BLOCKS):
-                for bank, acc in enumerate(accs):
-                    ob = first_block + bank
-                    nc.tensor.matmul(
-                        acc[:], w_sb[:, kb, ob * P : (ob + 1) * P], h_in[kb][:],
-                        start=(kb == 0), stop=(kb == HID_BLOCKS - 1),
-                    )
-            return accs
+                nc.tensor.matmul(
+                    acc[:], w_sb[:, kb, ob * P : (ob + 1) * P], h_in[kb][:],
+                    start=(kb == 0), stop=(kb == HID_BLOCKS - 1),
+                )
+            return acc
 
         def hidden_layer(layer, w_sb, h_in):
-            accs = dense(w_sb, 0, HID_BLOCKS, h_in)
-            return [sine(acc, layer * HID_BLOCKS + mb) for mb, acc in enumerate(accs)]
+            return [
+                sine(dense_block(w_sb, mb, h_in), layer * HID_BLOCKS + mb)
+                for mb in range(HID_BLOCKS)
+            ]
 
-        def store(piece, eb, acc, first, width):
-            column = SINE_LAYERS * HID_BLOCKS + eb
-            emb = work.tile([P, PIECE], F32, name="emb")
-            nc.vector.tensor_scalar(
-                emb[:, 0:width], acc[:, 0:width], bias_cols[:, column : column + 1], None,
-                op0=ADD,
-            )
-            token = piece * PIECE + first
-            nc.sync.dma_start(
-                out[eb * P : (eb + 1) * P, token : token + width], emb[:, 0:width]
-            )
-
-        def projection(piece, half, h_in, n_blocks=BLOCKS_A_HALF):
-            first_block = half * BLOCKS_A_HALF
-            if half == 0:
-                for bank, acc in enumerate(dense(wout_sb, first_block, BLOCKS_A_HALF, h_in)):
-                    store(piece, first_block + bank, acc, 0, PIECE)
-            else:
-                for eb in range(first_block, first_block + n_blocks):
-                    store(piece, eb, dense(wout_sb, eb, 1, h_in)[0], 0, PIECE)
-
-        def last_block(piece, eb, h_in):
-            for first in range(0, PIECE, LAST_WIDTH):
-                acc = psum.tile([P, PIECE], F32, name="acc")
-                for kb in range(HID_BLOCKS):
-                    nc.tensor.matmul(
-                        acc[:, 0:LAST_WIDTH],
-                        wout_sb[:, kb, eb * P : (eb + 1) * P],
-                        h_in[kb][:, first : first + LAST_WIDTH],
-                        start=(kb == 0), stop=(kb == HID_BLOCKS - 1),
-                    )
-                store(piece, eb, acc, first, LAST_WIDTH)
+        def projection(piece, half, h_in):
+            for eb in range(half * BLOCKS_A_HALF, (half + 1) * BLOCKS_A_HALF):
+                acc = dense_block(wout_sb, eb, h_in)
+                column = SINE_LAYERS * HID_BLOCKS + eb
+                emb = work.tile([P, PIECE], F32, name="emb")
+                nc.vector.tensor_scalar(
+                    emb[:], acc[:], bias_cols[:, column : column + 1], None, op0=ADD
+                )
+                nc.sync.dma_start(
+                    out[eb * P : (eb + 1) * P, piece * PIECE : (piece + 1) * PIECE], emb[:]
+                )
 
         h = {}
         for piece in (0, 1):
@@ -162,5 +140,4 @@ def tile_implicitembedding_b_kernel(
         h[3] = hidden_layer(2, w2_sb, h[3])
         projection(2, 1, h[2])
         projection(3, 0, h[3])
-        projection(3, 1, h[3], BLOCKS_A_HALF - 1)
-        last_block(3, EMB_BLOCKS - 1, h[3])
+        projection(3, 1, h[3])

@@ -16,7 +16,6 @@ HID_BLOCKS = HIDDEN // P
 EMB_BLOCKS = EMBED // P
 SINE_LAYERS = 3
 PSUM_BANKS = 8
-BLOCKS_A_HALF = EMB_BLOCKS // 2
 BIAS_ROWS = SINE_LAYERS * HID_BLOCKS + EMB_BLOCKS
 OMEGA0 = 30.0
 
@@ -108,8 +107,8 @@ def tile_implicitembedding_b_kernel(
                 for mb in range(HID_BLOCKS)
             ]
 
-        def projection(piece, half, h_in):
-            for eb in range(half * BLOCKS_A_HALF, (half + 1) * BLOCKS_A_HALF):
+        def projection(piece, h_in):
+            for eb in range(EMB_BLOCKS):
                 acc = dense_block(wout_sb, eb, h_in)
                 column = SINE_LAYERS * HID_BLOCKS + eb
                 emb = work.tile([P, PIECE], F32, name="emb")
@@ -120,24 +119,9 @@ def tile_implicitembedding_b_kernel(
                     out[eb * P : (eb + 1) * P, piece * PIECE : (piece + 1) * PIECE], emb[:]
                 )
 
-        h = {}
-        for piece in (0, 1):
-            h[piece] = first_layer(piece)
-        for piece in (0, 1):
-            h[piece] = hidden_layer(1, w1_sb, h[piece])
-        for piece in (0, 1):
-            h[piece] = hidden_layer(2, w2_sb, h[piece])
-        projection(0, 0, h[0])
-        for piece in (2, 3):
-            h[piece] = first_layer(piece)
-        projection(0, 1, h[0])
-        for piece in (2, 3):
-            h[piece] = hidden_layer(1, w1_sb, h[piece])
-        projection(1, 0, h[1])
-        h[2] = hidden_layer(2, w2_sb, h[2])
-        projection(1, 1, h[1])
-        projection(2, 0, h[2])
-        h[3] = hidden_layer(2, w2_sb, h[3])
-        projection(2, 1, h[2])
-        projection(3, 0, h[3])
-        projection(3, 1, h[3])
+        pieces = range(N_PIECES)
+        h = [first_layer(piece) for piece in pieces]
+        h = [hidden_layer(1, w1_sb, h[piece]) for piece in pieces]
+        h = [hidden_layer(2, w2_sb, h[piece]) for piece in pieces]
+        for piece in pieces:
+            projection(piece, h[piece])

@@ -17,6 +17,7 @@ EMB_BLOCKS = EMBED // P
 SINE_LAYERS = 3
 PSUM_BANKS = 8
 BIAS_ROWS = SINE_LAYERS * HID_BLOCKS + EMB_BLOCKS
+WARM_UP_MATMULS = 8
 OMEGA0 = 30.0
 
 FLOPS = 2 * TOKENS * (COORDS * HIDDEN + 2 * HIDDEN * HIDDEN + HIDDEN * EMBED)
@@ -55,6 +56,12 @@ def tile_implicitembedding_b_kernel(
         nc.sync.dma_start(w2_sb[:], w2.rearrange("(kb p) m -> p kb m", p=P))
         wout_sb = held.tile([P, HID_BLOCKS, EMBED], BF16, name="wout_sb")
         nc.sync.dma_start(wout_sb[:], wout.rearrange("(kb p) e -> p kb e", p=P))
+
+        zeros = held.tile([P, PIECE], BF16, name="zeros")
+        nc.vector.memset(zeros[:], 0.0)
+        warm = psum.tile([P, PIECE], F32, name="acc")
+        for repeat in range(WARM_UP_MATMULS):
+            nc.tensor.matmul(warm[:], zeros[:, 0:P], zeros[:], start=True, stop=True)
 
         identity = held.tile([BIAS_ROWS, BIAS_ROWS], F32, name="identity")
         make_identity(nc, identity[:])

@@ -1,5 +1,4 @@
 import concourse.mybir as mybir
-from concourse.masks import make_identity
 
 BF16 = mybir.dt.bfloat16
 F32 = mybir.dt.float32
@@ -16,8 +15,6 @@ HID_BLOCKS = HIDDEN // P
 EMB_BLOCKS = EMBED // P
 SINE_LAYERS = 3
 PSUM_BANKS = 8
-BIAS_ROWS = SINE_LAYERS * HID_BLOCKS + EMB_BLOCKS
-WARM_UP_MATMULS = 8
 OMEGA0 = 30.0
 
 FLOPS = 2 * TOKENS * (COORDS * HIDDEN + 2 * HIDDEN * HIDDEN + HIDDEN * EMBED)
@@ -33,16 +30,6 @@ def tile_implicitembedding_b_kernel(
         tc.tile_pool(name="work", bufs=PSUM_BANKS) as work,
         tc.psum_pool(name="psum", bufs=PSUM_BANKS) as psum,
     ):
-        bias_rows = held.tile([BIAS_ROWS, P], F32, name="bias_rows")
-        row = 0
-        for bias in (b0, b1, b2, bout):
-            blocks = bias.shape[0] // P
-            nc.sync.dma_start(
-                bias_rows[row : row + blocks, :],
-                bias.rearrange("(t p) one -> t (p one)", p=P),
-            )
-            row += blocks
-
         offsets = held.tile([P, TOKENS // 16], U16, name="offsets")
         nc.sync.dma_start(offsets[:], offs)
         table_sb = held.tile([P, WORDS], BF16, name="table_sb")
@@ -50,37 +37,36 @@ def tile_implicitembedding_b_kernel(
         w0_sb = held.tile([P, HIDDEN], BF16, name="w0_sb")
         nc.scalar.dma_start(w0_sb[:], w0)
 
+        b0_sb = held.tile([P, HID_BLOCKS], F32, name="b0_sb")
+        nc.scalar.dma_start(b0_sb[:], b0.rearrange("(p t) one -> p (t one)", t=HID_BLOCKS))
+        b1_sb = held.tile([P, HID_BLOCKS], F32, name="b1_sb")
+        nc.sync.dma_start(b1_sb[:], b1.rearrange("(p t) one -> p (t one)", t=HID_BLOCKS))
+        b2_sb = held.tile([P, HID_BLOCKS], F32, name="b2_sb")
+        nc.sync.dma_start(b2_sb[:], b2.rearrange("(p t) one -> p (t one)", t=HID_BLOCKS))
+        bout_sb = held.tile([P, EMB_BLOCKS], F32, name="bout_sb")
+        nc.sync.dma_start(
+            bout_sb[:], bout.rearrange("(p t) one -> p (t one)", t=EMB_BLOCKS)
+        )
+
         w1_sb = held.tile([P, HID_BLOCKS, HIDDEN], BF16, name="w1_sb")
-        nc.sync.dma_start(w1_sb[:], w1.rearrange("(kb p) m -> p kb m", p=P))
+        nc.sync.dma_start(w1_sb[:], w1.rearrange("(p kb) m -> p kb m", kb=HID_BLOCKS))
         w2_sb = held.tile([P, HID_BLOCKS, HIDDEN], BF16, name="w2_sb")
-        nc.sync.dma_start(w2_sb[:], w2.rearrange("(kb p) m -> p kb m", p=P))
+        nc.sync.dma_start(w2_sb[:], w2.rearrange("(p kb) m -> p kb m", kb=HID_BLOCKS))
         wout_sb = held.tile([P, HID_BLOCKS, EMBED], BF16, name="wout_sb")
-        nc.sync.dma_start(wout_sb[:], wout.rearrange("(kb p) e -> p kb e", p=P))
+        nc.sync.dma_start(wout_sb[:], wout.rearrange("(p kb) e -> p kb e", kb=HID_BLOCKS))
+        out_blocks = out.rearrange("(p t) n -> p t n", t=EMB_BLOCKS)
 
-        zeros = held.tile([P, PIECE], BF16, name="zeros")
-        nc.vector.memset(zeros[:], 0.0)
-        warm = psum.tile([P, PIECE], F32, name="acc")
-        for repeat in range(WARM_UP_MATMULS):
-            nc.tensor.matmul(warm[:], zeros[:, 0:P], zeros[:], start=True, stop=True)
+        omega_b = []
+        for layer, bias in enumerate((b0_sb, b1_sb, b2_sb)):
+            scaled = held.tile([P, HID_BLOCKS], F32, name=f"omega_b{layer}")
+            nc.vector.tensor_scalar(scaled[:], bias[:], OMEGA0, None, op0=MULT)
+            omega_b.append(scaled)
 
-        identity = held.tile([BIAS_ROWS, BIAS_ROWS], F32, name="identity")
-        make_identity(nc, identity[:])
-        flipped = psum.tile([P, PIECE], F32, name="acc")
-        nc.tensor.matmul(
-            flipped[:, 0:BIAS_ROWS], bias_rows[:], identity[:], start=True, stop=True
-        )
-        bias_cols = held.tile([P, BIAS_ROWS], F32, name="bias_cols")
-        nc.vector.tensor_copy(bias_cols[:], flipped[:, 0:BIAS_ROWS])
-        bias_times_omega = held.tile([P, BIAS_ROWS], F32, name="bias_times_omega")
-        nc.vector.tensor_scalar(
-            bias_times_omega[:], flipped[:, 0:BIAS_ROWS], OMEGA0, None, op0=MULT
-        )
-
-        def sine(acc, column):
+        def sine(acc, layer, t):
             h_block = hidden.tile([P, PIECE], BF16, name="h_block")
             nc.scalar.activation(
                 h_block[:], acc[:], SIN,
-                bias=bias_times_omega[:, column : column + 1], scale=OMEGA0,
+                bias=omega_b[layer][:, t : t + 1], scale=OMEGA0,
             )
             return h_block
 
@@ -90,40 +76,39 @@ def tile_implicitembedding_b_kernel(
                 acc = psum.tile([P, PIECE], F32, name="acc")
                 nc.tensor.matmul(
                     acc[:],
-                    w0_sb[:, mb * P : (mb + 1) * P],
+                    w0_sb[:, mb::HID_BLOCKS],
                     table_sb[:].indirect(
                         offsets[:, piece * (PIECE // 16) : (piece + 1) * (PIECE // 16)]
                     ),
                     start=True, stop=True,
                 )
-                h_out.append(sine(acc, mb))
+                h_out.append(sine(acc, 0, mb))
             return h_out
 
-        def dense_block(w_sb, ob, h_in):
+        def dense_block(w_sb, ob, blocks, h_in):
             acc = psum.tile([P, PIECE], F32, name="acc")
             for kb in range(HID_BLOCKS):
                 nc.tensor.matmul(
-                    acc[:], w_sb[:, kb, ob * P : (ob + 1) * P], h_in[kb][:],
+                    acc[:], w_sb[:, kb, ob::blocks], h_in[kb][:],
                     start=(kb == 0), stop=(kb == HID_BLOCKS - 1),
                 )
             return acc
 
         def hidden_layer(layer, w_sb, h_in):
             return [
-                sine(dense_block(w_sb, mb, h_in), layer * HID_BLOCKS + mb)
+                sine(dense_block(w_sb, mb, HID_BLOCKS, h_in), layer, mb)
                 for mb in range(HID_BLOCKS)
             ]
 
         def projection(piece, h_in):
             for eb in range(EMB_BLOCKS):
-                acc = dense_block(wout_sb, eb, h_in)
-                column = SINE_LAYERS * HID_BLOCKS + eb
+                acc = dense_block(wout_sb, eb, EMB_BLOCKS, h_in)
                 emb = work.tile([P, PIECE], F32, name="emb")
                 nc.vector.tensor_scalar(
-                    emb[:], acc[:], bias_cols[:, column : column + 1], None, op0=ADD
+                    emb[:], acc[:], bout_sb[:, eb : eb + 1], None, op0=ADD
                 )
                 nc.sync.dma_start(
-                    out[eb * P : (eb + 1) * P, piece * PIECE : (piece + 1) * PIECE], emb[:]
+                    out_blocks[:, eb, piece * PIECE : (piece + 1) * PIECE], emb[:]
                 )
 
         pieces = range(N_PIECES)

@@ -6,6 +6,7 @@ U16 = mybir.dt.uint16
 ADD = mybir.AluOpType.add
 MULT = mybir.AluOpType.mult
 SIN = mybir.ActivationFunctionType.Sin
+IDENTITY = mybir.ActivationFunctionType.Identity
 
 P = 128
 WORDS, COORDS, HIDDEN, EMBED, TOKENS = 4096, 128, 512, 1024, 2048
@@ -70,50 +71,62 @@ def tile_implicitembedding_b_kernel(
             )
             return h_block
 
-        def first_layer(piece):
+        pieces = range(N_PIECES)
+
+        def first_layer():
             h_out = []
             for mb in range(HID_BLOCKS):
-                acc = psum.tile([P, PIECE], F32, name="acc")
-                nc.tensor.matmul(
-                    acc[:],
-                    w0_sb[:, mb::HID_BLOCKS],
-                    table_sb[:].indirect(
-                        offsets[:, piece * (PIECE // 16) : (piece + 1) * (PIECE // 16)]
-                    ),
-                    start=True, stop=True,
-                )
-                h_out.append(sine(acc, 0, mb))
+                h_block = []
+                for piece in pieces:
+                    acc = psum.tile([P, PIECE], F32, name="acc")
+                    nc.tensor.matmul(
+                        acc[:],
+                        w0_sb[:, mb::HID_BLOCKS],
+                        table_sb[:].indirect(
+                            offsets[:, piece * (PIECE // 16) : (piece + 1) * (PIECE // 16)]
+                        ),
+                        start=True, stop=True,
+                    )
+                    h_block.append(sine(acc, 0, mb))
+                h_out.append(h_block)
             return h_out
 
-        def dense_block(w_sb, ob, blocks, h_in):
-            acc = psum.tile([P, PIECE], F32, name="acc")
+        def dense_block(w_sb, ob, blocks, h_in, group):
+            accs = [psum.tile([P, PIECE], F32, name="acc") for piece in group]
             for kb in range(HID_BLOCKS):
-                nc.tensor.matmul(
-                    acc[:], w_sb[:, kb, ob::blocks], h_in[kb][:],
-                    start=(kb == 0), stop=(kb == HID_BLOCKS - 1),
-                )
-            return acc
+                for acc, piece in zip(accs, group):
+                    nc.tensor.matmul(
+                        acc[:], w_sb[:, kb, ob::blocks], h_in[kb][piece][:],
+                        start=(kb == 0), stop=(kb == HID_BLOCKS - 1),
+                    )
+            return accs
 
         def hidden_layer(layer, w_sb, h_in):
             return [
-                sine(dense_block(w_sb, mb, HID_BLOCKS, h_in), layer, mb)
+                [
+                    sine(acc, layer, mb)
+                    for acc in dense_block(w_sb, mb, HID_BLOCKS, h_in, pieces)
+                ]
                 for mb in range(HID_BLOCKS)
             ]
 
-        def projection(piece, h_in):
-            for eb in range(EMB_BLOCKS):
-                acc = dense_block(wout_sb, eb, EMB_BLOCKS, h_in)
+        def store_block(eb, h_in, group):
+            accs = dense_block(wout_sb, eb, EMB_BLOCKS, h_in, group)
+            for acc, piece in zip(accs, group):
                 emb = work.tile([P, PIECE], F32, name="emb")
-                nc.vector.tensor_scalar(
-                    emb[:], acc[:], bout_sb[:, eb : eb + 1], None, op0=ADD
-                )
+                bias = bout_sb[:, eb : eb + 1]
+                if piece % 2 == 0:
+                    nc.vector.tensor_scalar(emb[:], acc[:], bias, None, op0=ADD)
+                else:
+                    nc.scalar.activation(emb[:], acc[:], IDENTITY, bias=bias)
                 nc.sync.dma_start(
                     out_blocks[:, eb, piece * PIECE : (piece + 1) * PIECE], emb[:]
                 )
 
-        pieces = range(N_PIECES)
-        h = [first_layer(piece) for piece in pieces]
-        h = [hidden_layer(1, w1_sb, h[piece]) for piece in pieces]
-        h = [hidden_layer(2, w2_sb, h[piece]) for piece in pieces]
+        h = first_layer()
+        h = hidden_layer(1, w1_sb, h)
+        h = hidden_layer(2, w2_sb, h)
+        for eb in range(EMB_BLOCKS - 1):
+            store_block(eb, h, pieces)
         for piece in pieces:
-            projection(piece, h[piece])
+            store_block(EMB_BLOCKS - 1, h, [piece])

@@ -91,42 +91,59 @@ def tile_implicitembedding_b_kernel(
                 h_out.append(h_block)
             return h_out
 
-        def dense_block(w_sb, ob, blocks, h_in, group):
-            accs = [psum.tile([P, PIECE], F32, name="acc") for piece in group]
+        def dense_block(w_sb, ob, blocks, h_in, spans):
+            accs = [psum.tile([P, PIECE], F32, name="acc") for span in spans]
             for kb in range(HID_BLOCKS):
-                for acc, piece in zip(accs, group):
+                for acc, (piece, cols) in zip(accs, spans):
                     nc.tensor.matmul(
-                        acc[:], w_sb[:, kb, ob::blocks], h_in[kb][piece][:],
+                        acc[:, 0 : cols.stop - cols.start],
+                        w_sb[:, kb, ob::blocks],
+                        h_in[kb][piece][:, cols],
                         start=(kb == 0), stop=(kb == HID_BLOCKS - 1),
                     )
             return accs
+
+        whole_pieces = [(piece, slice(0, PIECE)) for piece in pieces]
 
         def hidden_layer(layer, w_sb, h_in):
             return [
                 [
                     sine(acc, layer, mb)
-                    for acc in dense_block(w_sb, mb, HID_BLOCKS, h_in, pieces)
+                    for acc in dense_block(w_sb, mb, HID_BLOCKS, h_in, whole_pieces)
                 ]
                 for mb in range(HID_BLOCKS)
             ]
 
-        def store_block(eb, h_in, group):
-            accs = dense_block(wout_sb, eb, EMB_BLOCKS, h_in, group)
-            for acc, piece in zip(accs, group):
+        def add_bias(turn, emb, acc, eb):
+            bias = bout_sb[:, eb : eb + 1]
+            if turn % 2 == 0:
+                nc.vector.tensor_scalar(emb, acc, bias, None, op0=ADD)
+            else:
+                nc.scalar.activation(emb, acc, IDENTITY, bias=bias)
+
+        def store(eb, piece, emb):
+            nc.sync.dma_start(
+                out_blocks[:, eb, piece * PIECE : (piece + 1) * PIECE], emb[:]
+            )
+
+        def store_block(eb, h_in, spans):
+            accs = dense_block(wout_sb, eb, EMB_BLOCKS, h_in, spans)
+            for acc, (piece, cols) in zip(accs, spans):
                 emb = work.tile([P, PIECE], F32, name="emb")
-                bias = bout_sb[:, eb : eb + 1]
-                if piece % 2 == 0:
-                    nc.vector.tensor_scalar(emb[:], acc[:], bias, None, op0=ADD)
-                else:
-                    nc.scalar.activation(emb[:], acc[:], IDENTITY, bias=bias)
-                nc.sync.dma_start(
-                    out_blocks[:, eb, piece * PIECE : (piece + 1) * PIECE], emb[:]
-                )
+                add_bias(piece, emb[:], acc[:], eb)
+                store(eb, piece, emb)
 
         h = first_layer()
         h = hidden_layer(1, w1_sb, h)
         h = hidden_layer(2, w2_sb, h)
         for eb in range(EMB_BLOCKS - 1):
-            store_block(eb, h, pieces)
-        for piece in pieces:
-            store_block(EMB_BLOCKS - 1, h, [piece])
+            store_block(eb, h, whole_pieces)
+        last_block, last_piece = EMB_BLOCKS - 1, N_PIECES - 1
+        for span in whole_pieces[:-1]:
+            store_block(last_block, h, [span])
+        emb = work.tile([P, PIECE], F32, name="emb")
+        for half in range(2):
+            cols = slice(half * PIECE // 2, (half + 1) * PIECE // 2)
+            acc = dense_block(wout_sb, last_block, EMB_BLOCKS, h, [(last_piece, cols)])[0]
+            add_bias(half, emb[:, cols], acc[:, 0 : PIECE // 2], last_block)
+        store(last_block, last_piece, emb)

@@ -121,9 +121,10 @@ def tile_implicitembedding_b_kernel(
             else:
                 nc.scalar.activation(emb, acc, IDENTITY, bias=bias)
 
-        def store(eb, piece, emb):
+        def store(eb, piece, cols, emb):
+            first = piece * PIECE
             nc.sync.dma_start(
-                out_blocks[:, eb, piece * PIECE : (piece + 1) * PIECE], emb[:]
+                out_blocks[:, eb, first + cols.start : first + cols.stop], emb[:, cols]
             )
 
         def store_block(eb, h_in, spans):
@@ -131,7 +132,7 @@ def tile_implicitembedding_b_kernel(
             for acc, (piece, cols) in zip(accs, spans):
                 emb = work.tile([P, PIECE], F32, name="emb")
                 add_bias(piece, emb[:], acc[:], eb)
-                store(eb, piece, emb)
+                store(eb, piece, cols, emb)
 
         h = first_layer()
         h = hidden_layer(1, w1_sb, h)
@@ -141,9 +142,9 @@ def tile_implicitembedding_b_kernel(
         last_block, last_piece = EMB_BLOCKS - 1, N_PIECES - 1
         for span in whole_pieces[:-1]:
             store_block(last_block, h, [span])
-        emb = work.tile([P, PIECE], F32, name="emb")
         for half in range(2):
+            emb = work.tile([P, PIECE], F32, name="emb")
             cols = slice(half * PIECE // 2, (half + 1) * PIECE // 2)
             acc = dense_block(wout_sb, last_block, EMB_BLOCKS, h, [(last_piece, cols)])[0]
             add_bias(half, emb[:, cols], acc[:, 0 : PIECE // 2], last_block)
-        store(last_block, last_piece, emb)
+            store(last_block, last_piece, cols, emb)

@@ -33,9 +33,9 @@ def tile_implicitembedding_b_kernel(
     ):
         offsets = held.tile([P, TOKENS // 16], U16, name="offsets")
         nc.sync.dma_start(offsets[:], offs)
-        table_sb = held.tile([P, WORDS], BF16, name="table_sb")
+        table_sb = held.tile([P, WORDS], BF16, name="table_sb", tag="table_then_wout")
         nc.sync.dma_start(table_sb[:], table)
-        w0_sb = held.tile([P, HIDDEN], BF16, name="w0_sb")
+        w0_sb = held.tile([P, HIDDEN], BF16, name="w0_sb", tag="w0_then_w2")
         nc.scalar.dma_start(w0_sb[:], w0)
 
         b0_sb = held.tile([P, HID_BLOCKS], F32, name="b0_sb")
@@ -51,10 +51,6 @@ def tile_implicitembedding_b_kernel(
 
         w1_sb = held.tile([P, HID_BLOCKS, HIDDEN], BF16, name="w1_sb")
         nc.sync.dma_start(w1_sb[:], w1.rearrange("(p kb) m -> p kb m", kb=HID_BLOCKS))
-        w2_sb = held.tile([P, HID_BLOCKS, HIDDEN], BF16, name="w2_sb")
-        nc.sync.dma_start(w2_sb[:], w2.rearrange("(p kb) m -> p kb m", kb=HID_BLOCKS))
-        wout_sb = held.tile([P, HID_BLOCKS, EMBED], BF16, name="wout_sb")
-        nc.sync.dma_start(wout_sb[:], wout.rearrange("(p kb) e -> p kb e", kb=HID_BLOCKS))
         out_blocks = out.rearrange("(p t) n -> p t n", t=EMB_BLOCKS)
 
         omega_b = []
@@ -114,9 +110,9 @@ def tile_implicitembedding_b_kernel(
                 for mb in range(HID_BLOCKS)
             ]
 
-        def add_bias(turn, emb, acc, eb):
+        def add_bias(piece, emb, acc, eb):
             bias = bout_sb[:, eb : eb + 1]
-            if turn % 2 == 0:
+            if piece % 2 == 1:
                 nc.vector.tensor_scalar(emb, acc, bias, None, op0=ADD)
             else:
                 nc.scalar.activation(emb, acc, IDENTITY, bias=bias)
@@ -135,6 +131,10 @@ def tile_implicitembedding_b_kernel(
                 store(eb, piece, cols, emb)
 
         h = first_layer()
+        w2_sb = held.tile([P, HID_BLOCKS, HIDDEN], BF16, name="w2_sb", tag="w0_then_w2")
+        nc.sync.dma_start(w2_sb[:], w2.rearrange("(p kb) m -> p kb m", kb=HID_BLOCKS))
+        wout_sb = held.tile([P, HID_BLOCKS, EMBED], BF16, name="wout_sb", tag="table_then_wout")
+        nc.sync.dma_start(wout_sb[:], wout.rearrange("(p kb) e -> p kb e", kb=HID_BLOCKS))
         h = hidden_layer(1, w1_sb, h)
         h = hidden_layer(2, w2_sb, h)
         for eb in range(EMB_BLOCKS - 1):
@@ -146,5 +146,5 @@ def tile_implicitembedding_b_kernel(
             emb = work.tile([P, PIECE], F32, name="emb")
             cols = slice(half * PIECE // 2, (half + 1) * PIECE // 2)
             acc = dense_block(wout_sb, last_block, EMB_BLOCKS, h, [(last_piece, cols)])[0]
-            add_bias(half, emb[:, cols], acc[:, 0 : PIECE // 2], last_block)
+            add_bias(last_piece, emb[:, cols], acc[:, 0 : PIECE // 2], last_block)
             store(last_block, last_piece, cols, emb)

import concourse.mybir as mybir

BF16 = mybir.dt.bfloat16
F32 = mybir.dt.float32
U16 = mybir.dt.uint16
ADD = mybir.AluOpType.add
MULT = mybir.AluOpType.mult
SIN = mybir.ActivationFunctionType.Sin
IDENTITY = mybir.ActivationFunctionType.Identity

P = 128
WORDS, COORDS, HIDDEN, EMBED, TOKENS = 4096, 128, 512, 1024, 2048
PIECE = 512
N_PIECES = TOKENS // PIECE
HID_BLOCKS = HIDDEN // P
EMB_BLOCKS = EMBED // P
SINE_LAYERS = 3
PSUM_BANKS = 8
OMEGA0 = 30.0

FLOPS = 2 * TOKENS * (COORDS * HIDDEN + 2 * HIDDEN * HIDDEN + HIDDEN * EMBED)


def tile_implicitembedding_b_kernel(
    tc, table, w0, b0, w1, b1, w2, b2, wout, bout, offs, out
):
    nc = tc.nc
    with (
        tc.tile_pool(name="held", bufs=1) as held,
        tc.tile_pool(name="hidden", bufs=SINE_LAYERS * N_PIECES * HID_BLOCKS) as hidden,
        tc.tile_pool(name="work", bufs=PSUM_BANKS) as work,
        tc.psum_pool(name="psum", bufs=PSUM_BANKS) as psum,
    ):
        offsets = held.tile([P, TOKENS // 16], U16, name="offsets")
        nc.sync.dma_start(offsets[:], offs)
        table_sb = held.tile([P, WORDS], BF16, name="table_sb", tag="table_then_wout")
        nc.sync.dma_start(table_sb[:], table)
        w0_sb = held.tile([P, HIDDEN], BF16, name="w0_sb", tag="w0_then_w2")
        nc.scalar.dma_start(w0_sb[:], w0)

        b0_sb = held.tile([P, HID_BLOCKS], F32, name="b0_sb")
        nc.scalar.dma_start(b0_sb[:], b0.rearrange("(p t) one -> p (t one)", t=HID_BLOCKS))
        b1_sb = held.tile([P, HID_BLOCKS], F32, name="b1_sb")
        nc.sync.dma_start(b1_sb[:], b1.rearrange("(p t) one -> p (t one)", t=HID_BLOCKS))
        b2_sb = held.tile([P, HID_BLOCKS], F32, name="b2_sb")
        nc.sync.dma_start(b2_sb[:], b2.rearrange("(p t) one -> p (t one)", t=HID_BLOCKS))
        bout_sb = held.tile([P, EMB_BLOCKS], F32, name="bout_sb")
        nc.sync.dma_start(
            bout_sb[:], bout.rearrange("(p t) one -> p (t one)", t=EMB_BLOCKS)
        )

        w1_sb = held.tile([P, HID_BLOCKS, HIDDEN], BF16, name="w1_sb")
        nc.sync.dma_start(w1_sb[:], w1.rearrange("(p kb) m -> p kb m", kb=HID_BLOCKS))
        out_blocks = out.rearrange("(p t) n -> p t n", t=EMB_BLOCKS)

        omega_b = []
        for layer, bias in enumerate((b0_sb, b1_sb, b2_sb)):
            scaled = held.tile([P, HID_BLOCKS], F32, name=f"omega_b{layer}")
            nc.vector.tensor_scalar(scaled[:], bias[:], OMEGA0, None, op0=MULT)
            omega_b.append(scaled)

        def sine(acc, layer, t):
            h_block = hidden.tile([P, PIECE], BF16, name="h_block")
            nc.scalar.activation(
                h_block[:], acc[:], SIN,
                bias=omega_b[layer][:, t : t + 1], scale=OMEGA0,
            )
            return h_block

        pieces = range(N_PIECES)

        def first_layer():
            h_out = []
            for mb in range(HID_BLOCKS):
                h_block = []
                for piece in pieces:
                    acc = psum.tile([P, PIECE], F32, name="acc")
                    nc.tensor.matmul(
                        acc[:],
                        w0_sb[:, mb::HID_BLOCKS],
                        table_sb[:].indirect(
                            offsets[:, piece * (PIECE // 16) : (piece + 1) * (PIECE // 16)]
                        ),
                        start=True, stop=True,
                    )
                    h_block.append(sine(acc, 0, mb))
                h_out.append(h_block)
            return h_out

        def dense_block(w_sb, ob, blocks, h_in, spans):
            accs = [psum.tile([P, PIECE], F32, name="acc") for span in spans]
            for kb in range(HID_BLOCKS):
                for acc, (piece, cols) in zip(accs, spans):
                    nc.tensor.matmul(
                        acc[:, 0 : cols.stop - cols.start],
                        w_sb[:, kb, ob::blocks],
                        h_in[kb][piece][:, cols],
                        start=(kb == 0), stop=(kb == HID_BLOCKS - 1),
                    )
            return accs

        whole_pieces = [(piece, slice(0, PIECE)) for piece in pieces]

        def hidden_layer(layer, w_sb, h_in):
            return [
                [
                    sine(acc, layer, mb)
                    for acc in dense_block(w_sb, mb, HID_BLOCKS, h_in, whole_pieces)
                ]
                for mb in range(HID_BLOCKS)
            ]

        def add_bias(piece, emb, acc, eb):
            bias = bout_sb[:, eb : eb + 1]
            if piece % 2 == 1:
                nc.vector.tensor_scalar(emb, acc, bias, None, op0=ADD)
            else:
                nc.scalar.activation(emb, acc, IDENTITY, bias=bias)

        def store(eb, piece, cols, emb):
            first = piece * PIECE
            nc.sync.dma_start(
                out_blocks[:, eb, first + cols.start : first + cols.stop], emb[:, cols]
            )

        def store_block(eb, h_in, spans):
            accs = dense_block(wout_sb, eb, EMB_BLOCKS, h_in, spans)
            for acc, (piece, cols) in zip(accs, spans):
                emb = work.tile([P, PIECE], F32, name="emb")
                add_bias(piece, emb[:], acc[:], eb)
                store(eb, piece, cols, emb)

        h = first_layer()
        w2_sb = held.tile([P, HID_BLOCKS, HIDDEN], BF16, name="w2_sb", tag="w0_then_w2")
        nc.sync.dma_start(w2_sb[:], w2.rearrange("(p kb) m -> p kb m", kb=HID_BLOCKS))
        wout_sb = held.tile([P, HID_BLOCKS, EMBED], BF16, name="wout_sb", tag="table_then_wout")
        nc.sync.dma_start(wout_sb[:], wout.rearrange("(p kb) e -> p kb e", kb=HID_BLOCKS))
        h = hidden_layer(1, w1_sb, h)
        h = hidden_layer(2, w2_sb, h)
        for eb in range(EMB_BLOCKS - 1):
            store_block(eb, h, whole_pieces)
        last_block, last_piece = EMB_BLOCKS - 1, N_PIECES - 1
        for span in whole_pieces[:-1]:
            store_block(last_block, h, [span])
        for half in range(2):
            emb = work.tile([P, PIECE], F32, name="emb")
            cols = slice(half * PIECE // 2, (half + 1) * PIECE // 2)
            acc = dense_block(wout_sb, last_block, EMB_BLOCKS, h, [(last_piece, cols)])[0]
            add_bias(last_piece, emb[:, cols], acc[:, 0 : PIECE // 2], last_block)
            store(last_block, last_piece, cols, emb)
